import numpy as np
import ml_dtypes


def mxq(x, axis, fmt="e4m3"):
    dtype, down = {"e4m3": (ml_dtypes.float8_e4m3fn, 7), "e5m2": (ml_dtypes.float8_e5m2, 14)}[fmt]
    v = np.moveaxis(np.asarray(x, np.float32).astype(ml_dtypes.bfloat16).astype(np.float64), axis, -1)
    blocks = v.reshape(v.shape[:-1] + (-1, 32))
    amax = np.abs(blocks).max(-1, keepdims=True)
    byte = np.maximum(np.where(amax > 0, np.frexp(amax)[1] - 1 + 127, 0) - down, 1)
    scale = np.exp2(byte - 127.0)
    codes = (blocks / scale).astype(np.float32).astype(dtype).astype(np.float64)
    return np.moveaxis((codes * scale).reshape(v.shape), -1, axis)


WIDE = False


def mx_kscale(k):
    if not WIDE:
        return np.ones(k)
    levels = np.array([10, -10, 5, -5, 0])
    if k % 512:
        return np.exp2(np.random.permutation(np.resize(levels, k // 32))).repeat(32)
    a = np.empty((k // 512, 16))
    for p in range(k // 512):
        a[p, :8] = np.random.permutation(np.resize(levels, 8))
        for g in range(8):
            far = levels[np.abs(levels - a[p, g]) >= 10]
            a[p, g + 8] = far[np.random.randint(len(far))]
    return np.exp2(a.ravel()).repeat(32)


BF16 = ml_dtypes.bfloat16


def bf(x):
    return np.asarray(x, np.float32).astype(BF16)


def f64(x):
    return np.asarray(x).astype(np.float64)


B, N, E, H, NOPE, VDIM, ROPE, QR, KVR = 4, 1024, 1024, 4, 64, 128, 32, 512, 512
QH = NOPE + ROPE
BASE = 10000.0


def rope(v):
    d = v.shape[-1]
    n = v.shape[-2]
    theta = BASE ** (-2.0 * np.arange(d // 2) / d)
    ang = np.arange(n)[:, None] * theta[None, :]
    cos, sin = np.cos(ang), np.sin(ang)
    v1, v2 = v[..., 0::2], v[..., 1::2]
    return np.stack([v1 * cos - v2 * sin, v1 * sin + v2 * cos], axis=-1).reshape(v.shape)


def draw0():
    s, t = mx_kscale(E), mx_kscale(QR)
    return {"x": bf(np.random.standard_normal((B, N, E)) * s),
            "Wqa": bf(np.random.standard_normal((E, QR)) / np.sqrt(E) / s[:, None] * t),
            "Wqb": bf(np.random.standard_normal((QR, H * QH)) / np.sqrt(QR) / t[:, None])}


def core(x, Wqa, Wqb):
    cq = mxq(f64(x), 2, "e4m3") @ mxq(f64(Wqa), 0, "e4m3")
    q = mxq(cq, 2, "e4m3") @ mxq(f64(Wqb), 0, "e4m3")
    q = q.reshape(B, N, H, QH).transpose(0, 2, 1, 3)
    return np.concatenate([q[..., :NOPE], rope(q[..., NOPE:])], axis=-1)


def e4m3fn_bytes(y):
    return np.clip(np.asarray(y, np.float64), -448.0, 448.0).astype(np.float32).astype(ml_dtypes.float8_e4m3fn).view(np.uint8)


def e4m3fn_values(b):
    return np.asarray(b, np.uint8).view(ml_dtypes.float8_e4m3fn).astype(np.float64)


def setup_inputs():
    d = draw0()
    x0 = np.asarray(d['x']).astype(np.float64)
    s = (np.max(np.abs(x0), axis=(0, 1), keepdims=True) / 448.0).astype(np.float32)
    out = {}
    for k, v in d.items():
        if k == 'x':
            out['x_bytes'] = e4m3fn_bytes(x0 / s.astype(np.float64))
            out['x_scale'] = s
        else:
            out[k] = v
    return out


def reference(x_bytes, x_scale, Wqa, Wqb):
    return core(e4m3fn_values(x_bytes) * x_scale.astype(np.float64), Wqa, Wqb)

@@ -1,0 +1,334 @@
+import math
+from contextlib import ExitStack
+
+import concourse.mybir as mybir
+from concourse.masks import make_identity
+
+B, N, E, H, NOPE, ROPE, QR = 4, 1024, 1024, 4, 64, 32, 512
+QH = NOPE + ROPE
+BASE = 10000.0
+FLOPS = 2 * B * N * E * QR + 2 * B * N * QR * H * QH + 6 * B * N * H * ROPE // 2
+
+F32 = mybir.dt.float32
+BF16 = mybir.dt.bfloat16
+I32 = mybir.dt.int32
+U32 = mybir.dt.uint32
+U8 = mybir.dt.uint8
+F8 = mybir.dt.float8_e4m3fn
+F8X4 = mybir.dt.float8_e4m3fn_x4
+ALU = mybir.AluOpType
+ACT = mybir.ActivationFunctionType
+
+P = 128
+J = N // P
+PAIRS = B * J // 2
+TILES = B * J
+AHEAD = 3
+
+
+def kind_of(q):
+    if q >= 8 and q % 3 == 2:
+        return "pre"
+    if q >= 8 and q % 4 == 0:
+        return "vec"
+    return "act"
+
+
+def tile_multilatentattention_pa_t_kernel(tc, x_bytes, x_scale, Wqa, Wqb, out):
+    nc = tc.nc
+    with ExitStack() as ctx:
+        keep = ctx.enter_context(tc.tile_pool(name="keep", bufs=1))
+        work = ctx.enter_context(tc.tile_pool(name="work", bufs=2))
+        psum = ctx.enter_context(tc.psum_pool(name="psum", bufs=2))
+
+        scale_k = keep.tile([P, 2, 4], F32, name="scale_k")
+        xb = []
+        for hb in range(2 * B):
+            xb.append(keep.tile([P, 4, E], U8, name="xb%d" % hb, align_bytes=64))
+
+        def load_x(hb, lo, hi):
+            src = x_bytes[hb // 2].rearrange("(p j) k -> p j k", j=J)
+            first = 4 * (hb % 2)
+            nc.sync.dma_start(out=xb[hb][:, lo:hi, :], in_=src[:, first + lo : first + hi, :])
+
+        wa_raw = keep.tile([P, 2, 4, QR], BF16, name="wa_raw", align_bytes=64)
+        wb_raw = keep.tile([P, 4, H * QH], BF16, name="wb_raw", align_bytes=64)
+        wa_src = Wqa.rearrange("(g p j) c -> g p j c", p=P, j=4)
+        load_x(0, 0, 2)
+        nc.sync.dma_start(out=scale_k[:], in_=x_scale.rearrange("a b (g p t) -> p (a b g) t", g=2, t=4))
+        nc.sync.dma_start(out=wa_raw[:, 0], in_=wa_src[0])
+        nc.sync.dma_start(out=wa_raw[:, 1], in_=wa_src[1])
+        load_x(0, 2, 4)
+        load_x(1, 0, 4)
+        nc.sync.dma_start(out=wb_raw[:], in_=Wqb.rearrange("(p j) c -> p j c", j=4))
+        scale_b = keep.tile([P, E], F32, name="scale_b", align_bytes=64)
+        load_x(2, 0, 4)
+        nc.sync.dma_start(out=scale_b[:], in_=x_scale.rearrange("a b k -> (a b k)").partition_broadcast(P))
+        for hb in range(3, 2 * B):
+            load_x(hb, 0, 4)
+
+        pos = keep.tile([P, J], F32, name="pos")
+        ident = keep.tile([P, P], F32, name="ident", align_bytes=64)
+        turns = keep.tile([P, J, 16], F32, name="turns")
+        whole_i = keep.tile([P, J, 16], I32, name="whole_i")
+        whole = keep.tile([P, J, 16], F32, name="whole")
+        frac = keep.tile([P, J, 16], F32, name="frac")
+        comp = keep.tile([P, J, 16], F32, name="comp")
+        comp2 = keep.tile([P, J, 16], F32, name="comp2")
+        half_sin = keep.tile([P, J, 16], F32, name="half_sin")
+        half_cos = keep.tile([P, J, 16], F32, name="half_cos")
+        sc = keep.tile([P, J, 16], F32, name="sc")
+        ss = keep.tile([P, J, 16], F32, name="ss")
+        cos_t = keep.tile([P, J, 16, 2], F32, name="cos_t")
+        sin_t = keep.tile([P, J, 16, 2], F32, name="sin_t")
+
+        wa_grp = keep.tile([P, 2, 2048], BF16, name="wa_grp", align_bytes=64)
+        wa_codes = keep.tile([P, 2, QR], U32, name="wa_codes", align_bytes=64)
+        wa_scales = keep.tile([P, 2, QR], U8, name="wa_scales", align_bytes=64)
+        wb_grp = keep.tile([P, H * QH * 4], BF16, name="wb_grp", align_bytes=64)
+        wb_codes = keep.tile([P, H * QH], U32, name="wb_codes", align_bytes=64)
+        wb_scales = keep.tile([P, H * QH], U8, name="wb_scales", align_bytes=64)
+
+        def group_wa(g):
+            dst = wa_grp[:, g, :].rearrange("p (t m j) -> p t m j", t=4, j=4)
+            src = wa_raw[:, g].rearrange("p j (m t) -> p t m j", t=4)
+            if g == 0:
+                nc.vector.tensor_copy(out=dst, in_=src)
+            else:
+                nc.gpsimd.tensor_scalar(out=dst, in0=src, scalar1=1.0, scalar2=0.0, op0=ALU.mult, op1=ALU.add)
+
+        def quant_wa(g):
+            nc.vector.quantize_mx(out=wa_codes[:, g, :].bitcast(F8X4), scales=wa_scales[:, g, :], in_=wa_grp[:, g, :])
+
+        def group_wb():
+            raw = wb_raw[:].rearrange("p j (h f) -> p h f j", h=H)
+            nc.gpsimd.tensor_scalar(out=wb_grp[:, 0:1024].rearrange("p (h f j) -> p h f j", h=H, j=4), in0=raw[:, :, 0:NOPE, :], scalar1=1.0, scalar2=0.0, op0=ALU.mult, op1=ALU.add)
+            nc.gpsimd.tensor_scalar(out=wb_grp[:, 1024:1536].rearrange("p (h f j) -> p h f j", h=H, j=4), in0=raw[:, :, NOPE:QH, :], scalar1=1.0, scalar2=0.0, op0=ALU.mult, op1=ALU.add)
+
+        def quant_wb():
+            nc.vector.quantize_mx(out=wb_codes[:, 0:256].bitcast(F8X4), scales=wb_scales[:, 0:256], in_=wb_grp[:, 0:1024])
+            nc.vector.quantize_mx(out=wb_codes[:, 256:384].bitcast(F8X4), scales=wb_scales[:, 256:384], in_=wb_grp[:, 1024:1536])
+
+        xs, xt, xc, cg, cc, nope_ps, rope_ps, rot, outs, banks, rope_sb = {}, {}, {}, {}, {}, {}, {}, {}, {}, {}, {}
+
+        def product(p, i):
+            q = 2 * p + i
+            t = work.tile([P, E], BF16, name="xs", bufs=2 * AHEAD + 4, align_bytes=64)
+            xs[q] = t
+            raw = xb[p // 2][:, 2 * (p % 2) + i, :].bitcast(F8)
+            if kind_of(q) == "pre":
+                nc.vector.tensor_tensor(out=t[:], in0=raw, in1=scale_b[:], op=ALU.mult)
+            elif kind_of(q) == "vec":
+                nc.vector.tensor_copy(out=t[:], in_=raw)
+            elif kind_of(q) == "pool":
+                nc.gpsimd.tensor_copy(out=t[:], in_=raw)
+            else:
+                nc.scalar.copy(out=t[:], in_=raw)
+
+        def turn(p, i):
+            q = 2 * p + i
+            if i == 0:
+                grouped = work.tile([P, 2, E], BF16, name="xt", bufs=3, align_bytes=64)
+                xt[p] = grouped
+            words = xs.pop(q)[:].bitcast(F32)
+            bank = psum.tile([P, 512], F32, name="tp", bufs=4)
+            for g in range(2):
+                for u in range(2):
+                    nc.tensor.transpose(
+                        bank[:, 128 * (2 * g + u) : 128 * (2 * g + u + 1)],
+                        words[:, 256 * g + u : 256 * (g + 1) : 2],
+                        ident[:],
+                    )
+            banks[q] = bank
+
+        def empty(p, i):
+            q = 2 * p + i
+            bank = banks.pop(q)
+            dst = xt[p][:, i, :]
+            if kind_of(q) == "pre":
+                nc.scalar.copy(
+                    out=dst.bitcast(F32).rearrange("p (g n u) -> p g n u", g=2, u=2),
+                    in_=bank[:].rearrange("p (g u n) -> p g n u", g=2, u=2),
+                )
+            else:
+                for g in range(2):
+                    nc.vector.tensor_tensor(
+                        out=dst.rearrange("p (g n u e) -> p g n u e", g=2, u=2, e=2)[:, g],
+                        in0=bank[:].bitcast(BF16).rearrange("p (g u n e) -> p g n u e", g=2, u=2, e=2)[:, g],
+                        in1=scale_k[:, g].rearrange("p (u e) -> p u e", u=2).unsqueeze(1).to_broadcast([P, P, 2, 2]),
+                        op=ALU.mult,
+                    )
+
+        def quant_x(p):
+            codes = work.tile([P, 512], U32, name="xc", bufs=3, align_bytes=64)
+            scales = work.tile([P, 512], U8, name="xcs", bufs=3, align_bytes=64)
+            xc[p] = (codes, scales)
+            nc.vector.quantize_mx(out=codes[:].bitcast(F8X4), scales=scales[:], in_=xt.pop(p)[:].rearrange("p i k -> p (i k)"))
+
+        def first_matmul(p):
+            codes, scales = xc.pop(p)
+            grouped = work.tile([P, 2, 512], BF16, name="cg", bufs=3, align_bytes=64)
+            cg[p] = grouped
+            for i in range(2):
+                bank = psum.tile([P, 512], F32, name="mm1")
+                for t in range(4):
+                    for g in range(2):
+                        w = slice(128 * t, 128 * (t + 1))
+                        c = slice(256 * i + 128 * g, 256 * i + 128 * (g + 1))
+                        nc.tensor.matmul_mx(
+                            out=bank[:, 128 * t : 128 * (t + 1)],
+                            lhsT=wa_codes[:, g, w].bitcast(F8X4),
+                            lhsT_scale=wa_scales[:, g, w],
+                            rhs=codes[:, c].bitcast(F8X4),
+                            rhs_scale=scales[:, c],
+                            start=(g == 0),
+                            stop=(g == 1),
+                        )
+                nc.scalar.copy(
+                    out=grouped[:, i, :].rearrange("p (n t) -> p n t", t=4),
+                    in_=bank[:].rearrange("p (t n) -> p n t", t=4),
+                )
+
+        def quant_c(p):
+            codes = work.tile([P, 256], U32, name="cc", bufs=3, align_bytes=64)
+            scales = work.tile([P, 256], U8, name="ccs", bufs=3, align_bytes=64)
+            cc[p] = (codes, scales)
+            nc.vector.quantize_mx(out=codes[:].bitcast(F8X4), scales=scales[:], in_=cg.pop(p)[:].rearrange("p i k -> p (i k)"))
+
+        def second_matmul(p):
+            codes, scales = cc.pop(p)
+            nb = psum.tile([P, 512], F32, name="nope", bufs=1)
+            rb = psum.tile([P, 256], F32, name="rope", bufs=1)
+            nope_ps[p], rope_ps[p] = nb, rb
+            for bank, width, first in ((nb, 256, 0), (rb, 128, 256)):
+                for i in range(2):
+                    t = slice(128 * i, 128 * (i + 1))
+                    w = slice(first, first + width)
+                    nc.tensor.matmul_mx(
+                        out=bank[:, width * i : width * (i + 1)],
+                        lhsT=codes[:, t].bitcast(F8X4),
+                        lhsT_scale=scales[:, t],
+                        rhs=wb_codes[:, w].bitcast(F8X4),
+                        rhs_scale=wb_scales[:, w],
+                        start=True,
+                        stop=True,
+                    )
+
+        def out_tile(p):
+            if p // 2 not in outs:
+                o = work.tile([P, H, 4, QH], F32, name="o", bufs=3, align_bytes=64)
+                outs[p // 2] = o
+            return outs[p // 2]
+
+        def nope_out(p):
+            jj = 2 * (p % 2)
+            nc.scalar.copy(
+                out=out_tile(p)[:, :, jj : jj + 2, 0:NOPE].rearrange("p h j f -> p j h f"),
+                in_=nope_ps.pop(p)[:].rearrange("p (j h f) -> p j h f", j=2, h=H),
+            )
+
+        def rope_on_vector(p):
+            return p >= PAIRS - 2
+
+        def rope_get(p):
+            if rope_on_vector(p):
+                rope_sb[p] = rope_ps.pop(p)
+            else:
+                r = work.tile([P, 256], F32, name="rsb", bufs=3)
+                nc.scalar.copy(out=r[:], in_=rope_ps.pop(p)[:])
+                rope_sb[p] = r
+
+        def rope_mul(p):
+            eng = nc.vector if rope_on_vector(p) else nc.gpsimd
+            j0 = 2 * (p % 4)
+            q = rope_sb.pop(p)[:].rearrange("p (j h f) -> p j h f", j=2, h=H)
+            parts = []
+            for name, table in (("rc", cos_t), ("rs", sin_t)):
+                t = work.tile([P, 256], F32, name=name, bufs=3)
+                tab = table[:, j0 : j0 + 2].rearrange("p j i e -> p j (i e)").unsqueeze(2).to_broadcast([P, 2, H, ROPE])
+                eng.tensor_tensor(out=t[:].rearrange("p (j h f) -> p j h f", j=2, h=H), in0=q, in1=tab, op=ALU.mult)
+                parts.append(t)
+            rot[p] = parts
+
+        def rope_add(p):
+            eng = nc.vector if rope_on_vector(p) else nc.gpsimd
+            jj = 2 * (p % 2)
+            rc, rs = rot.pop(p)
+            eng.tensor_tensor(
+                out=out_tile(p)[:, :, jj : jj + 2, NOPE:QH].rearrange("p h j (i e) -> p j h i e", e=2),
+                in0=rc[:].rearrange("p (j h i e) -> p j h i e", j=2, h=H, e=2),
+                in1=rs[:].rearrange("p (j h i e) -> p j h i e", j=2, h=H, e=2)[:, :, :, :, ::-1],
+                op=ALU.add,
+            )
+
+        def store(p):
+            b, half = p // 4, (p // 2) % 2
+            dst = out[b].rearrange("h (p j) f -> p h j f", j=J)[:, :, 4 * half : 4 * half + 4, :]
+            nc.sync.dma_start(out=dst, in_=outs.pop(p // 2)[:])
+
+        def tables_a():
+            nc.gpsimd.iota(pos[:], pattern=[[1, J]], base=0, channel_multiplier=J, allow_small_or_imprecise_dtypes=True)
+            make_identity(nc, ident[:])
+            for i in range(16):
+                theta = BASE ** (-2.0 * i / ROPE)
+                nc.vector.tensor_scalar(out=turns[:, :, i], in0=pos[:], scalar1=theta / (2.0 * math.pi), scalar2=None, op0=ALU.mult)
+            nc.vector.tensor_copy(out=whole_i[:], in_=turns[:])
+            nc.vector.tensor_copy(out=whole[:], in_=whole_i[:])
+            nc.vector.tensor_tensor(out=frac[:], in0=turns[:], in1=whole[:], op=ALU.subtract)
+            nc.vector.scalar_tensor_tensor(out=comp[:], in0=frac[:], scalar=-1.0, in1=frac[:], op0=ALU.mult, op1=ALU.max)
+            nc.vector.tensor_scalar(out=comp2[:], in0=comp[:], scalar1=-1.0, scalar2=0.5, op0=ALU.mult, op1=ALU.add)
+            nc.scalar.activation(out=half_sin[:], in_=frac[:], func=ACT.Sin, scale=math.pi)
+            nc.scalar.activation(out=half_cos[:], in_=comp2[:], func=ACT.Sin, scale=math.pi)
+
+        def tables_b():
+            nc.gpsimd.tensor_tensor(out=sc[:], in0=half_sin[:], in1=half_cos[:], op=ALU.mult)
+            nc.gpsimd.tensor_tensor(out=ss[:], in0=half_sin[:], in1=half_sin[:], op=ALU.mult)
+            for e in range(2):
+                nc.gpsimd.tensor_scalar(out=sin_t[:, :, :, e], in0=sc[:], scalar1=2.0 - 4.0 * e, scalar2=0.0, op0=ALU.mult, op1=ALU.add)
+                nc.gpsimd.tensor_scalar(out=cos_t[:, :, :, e], in0=ss[:], scalar1=-2.0, scalar2=1.0, op0=ALU.mult, op1=ALU.add)
+
+        def main():
+            tables_a()
+            for p in range(AHEAD):
+                for i in range(2):
+                    product(p, i)
+            group_wa(0)
+            group_wa(1)
+            tables_b()
+            group_wb()
+            turn(0, 0)
+            turn(0, 1)
+            for s in range(PAIRS + 4):
+                if s == 1:
+                    quant_wa(0)
+                    quant_wa(1)
+                if s == 2:
+                    quant_wb()
+                if s + 1 < PAIRS:
+                    turn(s + 1, 0)
+                    turn(s + 1, 1)
+                if s < PAIRS:
+                    empty(s, 0)
+                if s + AHEAD < PAIRS:
+                    product(s + AHEAD, 0)
+                if 0 <= s - 1 < PAIRS:
+                    quant_x(s - 1)
+                if 0 <= s - 3 < PAIRS:
+                    nope_out(s - 3)
+                    rope_get(s - 3)
+                    rope_mul(s - 3)
+                    rope_add(s - 3)
+                    if (s - 3) % 2 == 1:
+                        store(s - 3)
+                if s < PAIRS:
+                    empty(s, 1)
+                if s + AHEAD < PAIRS:
+                    product(s + AHEAD, 1)
+                if 0 <= s - 1 < PAIRS:
+                    first_matmul(s - 1)
+                if 0 <= s - 2 < PAIRS:
+                    quant_c(s - 2)
+                    second_matmul(s - 2)
+
+        with tc.manual_schedule():
+            main()

@@ -22,15 +22,15 @@ ACT = mybir.ActivationFunctionType
 P = 128
 J = N // P
 PAIRS = B * J // 2
-TILES = B * J
-AHEAD = 3
+SB = 4
+SPLIT = (PAIRS - 1,)
 
 
 def kind_of(q):
-    if q >= 8 and q % 3 == 2:
+    if q < 4:
+        return "vec" if q % 2 == 0 else "act"
+    if q >= 10 and q % 8 == 2:
         return "pre"
-    if q >= 8 and q % 4 == 0:
-        return "vec"
     return "act"
 
 
@@ -41,7 +41,6 @@ def tile_multilatentattention_pa_t_kernel(tc, x_bytes, x_scale, Wqa, Wqb, out):
         work = ctx.enter_context(tc.tile_pool(name="work", bufs=2))
         psum = ctx.enter_context(tc.psum_pool(name="psum", bufs=2))
 
-        scale_k = keep.tile([P, 2, 4], F32, name="scale_k")
         xb = []
         for hb in range(2 * B):
             xb.append(keep.tile([P, 4, E], U8, name="xb%d" % hb, align_bytes=64))
@@ -54,14 +53,16 @@ def tile_multilatentattention_pa_t_kernel(tc, x_bytes, x_scale, Wqa, Wqb, out):
         wa_raw = keep.tile([P, 2, 4, QR], BF16, name="wa_raw", align_bytes=64)
         wb_raw = keep.tile([P, 4, H * QH], BF16, name="wb_raw", align_bytes=64)
         wa_src = Wqa.rearrange("(g p j) c -> g p j c", p=P, j=4)
-        load_x(0, 0, 2)
+        scale_k = keep.tile([P, 2, 4], F32, name="scale_k")
+        scale_b = keep.tile([P, E], F32, name="scale_b", align_bytes=64)
+        load_x(0, 0, 1)
+        load_x(0, 1, 2)
         nc.sync.dma_start(out=scale_k[:], in_=x_scale.rearrange("a b (g p t) -> p (a b g) t", g=2, t=4))
         nc.sync.dma_start(out=wa_raw[:, 0], in_=wa_src[0])
-        nc.sync.dma_start(out=wa_raw[:, 1], in_=wa_src[1])
         load_x(0, 2, 4)
+        nc.sync.dma_start(out=wa_raw[:, 1], in_=wa_src[1])
         load_x(1, 0, 4)
         nc.sync.dma_start(out=wb_raw[:], in_=Wqb.rearrange("(p j) c -> p j c", j=4))
-        scale_b = keep.tile([P, E], F32, name="scale_b", align_bytes=64)
         load_x(2, 0, 4)
         nc.sync.dma_start(out=scale_b[:], in_=x_scale.rearrange("a b k -> (a b k)").partition_broadcast(P))
         for hb in range(3, 2 * B):
@@ -79,194 +80,9 @@ def tile_multilatentattention_pa_t_kernel(tc, x_bytes, x_scale, Wqa, Wqb, out):
         half_cos = keep.tile([P, J, 16], F32, name="half_cos")
         sc = keep.tile([P, J, 16], F32, name="sc")
         ss = keep.tile([P, J, 16], F32, name="ss")
-        cos_t = keep.tile([P, J, 16, 2], F32, name="cos_t")
-        sin_t = keep.tile([P, J, 16, 2], F32, name="sin_t")
+        table = keep.tile([P, J // 2, 2, 2 * H * ROPE], F32, name="table", align_bytes=64)
 
-        wa_grp = keep.tile([P, 2, 2048], BF16, name="wa_grp", align_bytes=64)
-        wa_codes = keep.tile([P, 2, QR], U32, name="wa_codes", align_bytes=64)
-        wa_scales = keep.tile([P, 2, QR], U8, name="wa_scales", align_bytes=64)
-        wb_grp = keep.tile([P, H * QH * 4], BF16, name="wb_grp", align_bytes=64)
-        wb_codes = keep.tile([P, H * QH], U32, name="wb_codes", align_bytes=64)
-        wb_scales = keep.tile([P, H * QH], U8, name="wb_scales", align_bytes=64)
-
-        def group_wa(g):
-            dst = wa_grp[:, g, :].rearrange("p (t m j) -> p t m j", t=4, j=4)
-            src = wa_raw[:, g].rearrange("p j (m t) -> p t m j", t=4)
-            if g == 0:
-                nc.vector.tensor_copy(out=dst, in_=src)
-            else:
-                nc.gpsimd.tensor_scalar(out=dst, in0=src, scalar1=1.0, scalar2=0.0, op0=ALU.mult, op1=ALU.add)
-
-        def quant_wa(g):
-            nc.vector.quantize_mx(out=wa_codes[:, g, :].bitcast(F8X4), scales=wa_scales[:, g, :], in_=wa_grp[:, g, :])
-
-        def group_wb():
-            raw = wb_raw[:].rearrange("p j (h f) -> p h f j", h=H)
-            nc.gpsimd.tensor_scalar(out=wb_grp[:, 0:1024].rearrange("p (h f j) -> p h f j", h=H, j=4), in0=raw[:, :, 0:NOPE, :], scalar1=1.0, scalar2=0.0, op0=ALU.mult, op1=ALU.add)
-            nc.gpsimd.tensor_scalar(out=wb_grp[:, 1024:1536].rearrange("p (h f j) -> p h f j", h=H, j=4), in0=raw[:, :, NOPE:QH, :], scalar1=1.0, scalar2=0.0, op0=ALU.mult, op1=ALU.add)
-
-        def quant_wb():
-            nc.vector.quantize_mx(out=wb_codes[:, 0:256].bitcast(F8X4), scales=wb_scales[:, 0:256], in_=wb_grp[:, 0:1024])
-            nc.vector.quantize_mx(out=wb_codes[:, 256:384].bitcast(F8X4), scales=wb_scales[:, 256:384], in_=wb_grp[:, 1024:1536])
-
-        xs, xt, xc, cg, cc, nope_ps, rope_ps, rot, outs, banks, rope_sb = {}, {}, {}, {}, {}, {}, {}, {}, {}, {}, {}
-
-        def product(p, i):
-            q = 2 * p + i
-            t = work.tile([P, E], BF16, name="xs", bufs=2 * AHEAD + 4, align_bytes=64)
-            xs[q] = t
-            raw = xb[p // 2][:, 2 * (p % 2) + i, :].bitcast(F8)
-            if kind_of(q) == "pre":
-                nc.vector.tensor_tensor(out=t[:], in0=raw, in1=scale_b[:], op=ALU.mult)
-            elif kind_of(q) == "vec":
-                nc.vector.tensor_copy(out=t[:], in_=raw)
-            elif kind_of(q) == "pool":
-                nc.gpsimd.tensor_copy(out=t[:], in_=raw)
-            else:
-                nc.scalar.copy(out=t[:], in_=raw)
-
-        def turn(p, i):
-            q = 2 * p + i
-            if i == 0:
-                grouped = work.tile([P, 2, E], BF16, name="xt", bufs=3, align_bytes=64)
-                xt[p] = grouped
-            words = xs.pop(q)[:].bitcast(F32)
-            bank = psum.tile([P, 512], F32, name="tp", bufs=4)
-            for g in range(2):
-                for u in range(2):
-                    nc.tensor.transpose(
-                        bank[:, 128 * (2 * g + u) : 128 * (2 * g + u + 1)],
-                        words[:, 256 * g + u : 256 * (g + 1) : 2],
-                        ident[:],
-                    )
-            banks[q] = bank
-
-        def empty(p, i):
-            q = 2 * p + i
-            bank = banks.pop(q)
-            dst = xt[p][:, i, :]
-            if kind_of(q) == "pre":
-                nc.scalar.copy(
-                    out=dst.bitcast(F32).rearrange("p (g n u) -> p g n u", g=2, u=2),
-                    in_=bank[:].rearrange("p (g u n) -> p g n u", g=2, u=2),
-                )
-            else:
-                for g in range(2):
-                    nc.vector.tensor_tensor(
-                        out=dst.rearrange("p (g n u e) -> p g n u e", g=2, u=2, e=2)[:, g],
-                        in0=bank[:].bitcast(BF16).rearrange("p (g u n e) -> p g n u e", g=2, u=2, e=2)[:, g],
-                        in1=scale_k[:, g].rearrange("p (u e) -> p u e", u=2).unsqueeze(1).to_broadcast([P, P, 2, 2]),
-                        op=ALU.mult,
-                    )
-
-        def quant_x(p):
-            codes = work.tile([P, 512], U32, name="xc", bufs=3, align_bytes=64)
-            scales = work.tile([P, 512], U8, name="xcs", bufs=3, align_bytes=64)
-            xc[p] = (codes, scales)
-            nc.vector.quantize_mx(out=codes[:].bitcast(F8X4), scales=scales[:], in_=xt.pop(p)[:].rearrange("p i k -> p (i k)"))
-
-        def first_matmul(p):
-            codes, scales = xc.pop(p)
-            grouped = work.tile([P, 2, 512], BF16, name="cg", bufs=3, align_bytes=64)
-            cg[p] = grouped
-            for i in range(2):
-                bank = psum.tile([P, 512], F32, name="mm1")
-                for t in range(4):
-                    for g in range(2):
-                        w = slice(128 * t, 128 * (t + 1))
-                        c = slice(256 * i + 128 * g, 256 * i + 128 * (g + 1))
-                        nc.tensor.matmul_mx(
-                            out=bank[:, 128 * t : 128 * (t + 1)],
-                            lhsT=wa_codes[:, g, w].bitcast(F8X4),
-                            lhsT_scale=wa_scales[:, g, w],
-                            rhs=codes[:, c].bitcast(F8X4),
-                            rhs_scale=scales[:, c],
-                            start=(g == 0),
-                            stop=(g == 1),
-                        )
-                nc.scalar.copy(
-                    out=grouped[:, i, :].rearrange("p (n t) -> p n t", t=4),
-                    in_=bank[:].rearrange("p (t n) -> p n t", t=4),
-                )
-
-        def quant_c(p):
-            codes = work.tile([P, 256], U32, name="cc", bufs=3, align_bytes=64)
-            scales = work.tile([P, 256], U8, name="ccs", bufs=3, align_bytes=64)
-            cc[p] = (codes, scales)
-            nc.vector.quantize_mx(out=codes[:].bitcast(F8X4), scales=scales[:], in_=cg.pop(p)[:].rearrange("p i k -> p (i k)"))
-
-        def second_matmul(p):
-            codes, scales = cc.pop(p)
-            nb = psum.tile([P, 512], F32, name="nope", bufs=1)
-            rb = psum.tile([P, 256], F32, name="rope", bufs=1)
-            nope_ps[p], rope_ps[p] = nb, rb
-            for bank, width, first in ((nb, 256, 0), (rb, 128, 256)):
-                for i in range(2):
-                    t = slice(128 * i, 128 * (i + 1))
-                    w = slice(first, first + width)
-                    nc.tensor.matmul_mx(
-                        out=bank[:, width * i : width * (i + 1)],
-                        lhsT=codes[:, t].bitcast(F8X4),
-                        lhsT_scale=scales[:, t],
-                        rhs=wb_codes[:, w].bitcast(F8X4),
-                        rhs_scale=wb_scales[:, w],
-                        start=True,
-                        stop=True,
-                    )
-
-        def out_tile(p):
-            if p // 2 not in outs:
-                o = work.tile([P, H, 4, QH], F32, name="o", bufs=3, align_bytes=64)
-                outs[p // 2] = o
-            return outs[p // 2]
-
-        def nope_out(p):
-            jj = 2 * (p % 2)
-            nc.scalar.copy(
-                out=out_tile(p)[:, :, jj : jj + 2, 0:NOPE].rearrange("p h j f -> p j h f"),
-                in_=nope_ps.pop(p)[:].rearrange("p (j h f) -> p j h f", j=2, h=H),
-            )
-
-        def rope_on_vector(p):
-            return p >= PAIRS - 2
-
-        def rope_get(p):
-            if rope_on_vector(p):
-                rope_sb[p] = rope_ps.pop(p)
-            else:
-                r = work.tile([P, 256], F32, name="rsb", bufs=3)
-                nc.scalar.copy(out=r[:], in_=rope_ps.pop(p)[:])
-                rope_sb[p] = r
-
-        def rope_mul(p):
-            eng = nc.vector if rope_on_vector(p) else nc.gpsimd
-            j0 = 2 * (p % 4)
-            q = rope_sb.pop(p)[:].rearrange("p (j h f) -> p j h f", j=2, h=H)
-            parts = []
-            for name, table in (("rc", cos_t), ("rs", sin_t)):
-                t = work.tile([P, 256], F32, name=name, bufs=3)
-                tab = table[:, j0 : j0 + 2].rearrange("p j i e -> p j (i e)").unsqueeze(2).to_broadcast([P, 2, H, ROPE])
-                eng.tensor_tensor(out=t[:].rearrange("p (j h f) -> p j h f", j=2, h=H), in0=q, in1=tab, op=ALU.mult)
-                parts.append(t)
-            rot[p] = parts
-
-        def rope_add(p):
-            eng = nc.vector if rope_on_vector(p) else nc.gpsimd
-            jj = 2 * (p % 2)
-            rc, rs = rot.pop(p)
-            eng.tensor_tensor(
-                out=out_tile(p)[:, :, jj : jj + 2, NOPE:QH].rearrange("p h j (i e) -> p j h i e", e=2),
-                in0=rc[:].rearrange("p (j h i e) -> p j h i e", j=2, h=H, e=2),
-                in1=rs[:].rearrange("p (j h i e) -> p j h i e", j=2, h=H, e=2)[:, :, :, :, ::-1],
-                op=ALU.add,
-            )
-
-        def store(p):
-            b, half = p // 4, (p // 2) % 2
-            dst = out[b].rearrange("h (p j) f -> p h j f", j=J)[:, :, 4 * half : 4 * half + 4, :]
-            nc.sync.dma_start(out=dst, in_=outs.pop(p // 2)[:])
-
-        def tables_a():
+        def tables_start():
             nc.gpsimd.iota(pos[:], pattern=[[1, J]], base=0, channel_multiplier=J, allow_small_or_imprecise_dtypes=True)
             make_identity(nc, ident[:])
             for i in range(16):
@@ -280,55 +96,285 @@ def tile_multilatentattention_pa_t_kernel(tc, x_bytes, x_scale, Wqa, Wqb, out):
             nc.scalar.activation(out=half_sin[:], in_=frac[:], func=ACT.Sin, scale=math.pi)
             nc.scalar.activation(out=half_cos[:], in_=comp2[:], func=ACT.Sin, scale=math.pi)
 
-        def tables_b():
+        def tables_end():
             nc.gpsimd.tensor_tensor(out=sc[:], in0=half_sin[:], in1=half_cos[:], op=ALU.mult)
             nc.gpsimd.tensor_tensor(out=ss[:], in0=half_sin[:], in1=half_sin[:], op=ALU.mult)
             for e in range(2):
-                nc.gpsimd.tensor_scalar(out=sin_t[:, :, :, e], in0=sc[:], scalar1=2.0 - 4.0 * e, scalar2=0.0, op0=ALU.mult, op1=ALU.add)
-                nc.gpsimd.tensor_scalar(out=cos_t[:, :, :, e], in0=ss[:], scalar1=-2.0, scalar2=1.0, op0=ALU.mult, op1=ALU.add)
+                for d in range(2):
+                    for c, part, mul, add in ((0, ss, -2.0, 1.0), (1, sc, 2.0 - 4.0 * e, 0.0)):
+                        nc.gpsimd.tensor_scalar(
+                            out=table[:, :, c, :].rearrange("p m (d h i e) -> p d e m h i", d=2, h=H, e=2)[:, d, e],
+                            in0=part[:].rearrange("p (m d) i -> p d m i", d=2)[:, d].unsqueeze(2).to_broadcast([P, J // 2, H, 16]),
+                            scalar1=mul,
+                            scalar2=add,
+                            op0=ALU.mult,
+                            op1=ALU.add,
+                        )
+
+        wa_grp = keep.tile([P, 2, 2048], BF16, name="wa_grp", align_bytes=64)
+        wa_codes = keep.tile([P, 2, QR], U32, name="wa_codes", align_bytes=64)
+        wa_scales = keep.tile([P, 2, QR], U8, name="wa_scales", align_bytes=64)
+        wb_grp = keep.tile([P, H * QH * 4], BF16, name="wb_grp", align_bytes=64)
+        wb_codes = keep.tile([P, H * QH], U32, name="wb_codes", align_bytes=64)
+        wb_scales = keep.tile([P, H * QH], U8, name="wb_scales", align_bytes=64)
+
+        def copy_on(engine, dst, src):
+            if engine == "vector":
+                nc.vector.tensor_copy(out=dst, in_=src)
+            elif engine == "scalar":
+                nc.scalar.copy(out=dst, in_=src)
+            else:
+                nc.gpsimd.tensor_scalar(out=dst, in0=src, scalar1=1.0, scalar2=0.0, op0=ALU.mult, op1=ALU.add)
+
+        def group_wa(g, engine):
+            copy_on(
+                engine,
+                wa_grp[:, g, :].rearrange("p (t m j) -> p t m j", t=4, j=4),
+                wa_raw[:, g].rearrange("p j (m t) -> p t m j", t=4),
+            )
+
+        def quant_wa():
+            for g in range(2):
+                nc.vector.quantize_mx(out=wa_codes[:, g, :].bitcast(F8X4), scales=wa_scales[:, g, :], in_=wa_grp[:, g, :])
+
+        def group_wb(engine):
+            raw = wb_raw[:].rearrange("p j (h f) -> p h f j", h=H)
+            copy_on(engine, wb_grp[:, 0:1024].rearrange("p (h f j) -> p h f j", h=H, j=4), raw[:, :, 0:NOPE, :])
+            copy_on(engine, wb_grp[:, 1024:1536].rearrange("p (h f j) -> p h f j", h=H, j=4), raw[:, :, NOPE:QH, :])
+
+        def quant_wb():
+            nc.vector.quantize_mx(out=wb_codes[:, 0:256].bitcast(F8X4), scales=wb_scales[:, 0:256], in_=wb_grp[:, 0:1024])
+            nc.vector.quantize_mx(out=wb_codes[:, 256:384].bitcast(F8X4), scales=wb_scales[:, 256:384], in_=wb_grp[:, 1024:1536])
+
+        xs, banks, xt, xc, cg, cc, nope_ps, rope_ps, rope_sb, rot, outs = {}, {}, {}, {}, {}, {}, {}, {}, {}, {}, {}
+        m1 = {}
+
+        def widen(p, i):
+            if not 0 <= p < PAIRS:
+                return
+            q = 2 * p + i
+            t = work.tile([P, E], BF16, name="xs", bufs=12, align_bytes=64)
+            xs[q] = t
+            raw = xb[p // 2][:, 2 * (p % 2) + i, :].bitcast(F8)
+            if kind_of(q) == "pre":
+                nc.vector.tensor_tensor(out=t[:], in0=raw, in1=scale_b[:], op=ALU.mult)
+            elif kind_of(q) == "vec":
+                nc.vector.tensor_copy(out=t[:], in_=raw)
+            elif kind_of(q) == "pool":
+                nc.gpsimd.tensor_copy(out=t[:], in_=raw)
+            else:
+                nc.scalar.copy(out=t[:], in_=raw)
+
+        def turn(p, i):
+            if not 0 <= p < PAIRS:
+                return
+            q = 2 * p + i
+            words = xs.pop(q)[:].bitcast(F32)
+            bank = psum.tile([P, 512], F32, name="tp", bufs=4)
+            banks[q] = bank
+            for g in range(2):
+                for u in range(2):
+                    nc.tensor.transpose(
+                        bank[:, 128 * (2 * u + g) : 128 * (2 * u + g + 1)],
+                        words[:, 256 * g + u : 256 * (g + 1) : 2],
+                        ident[:],
+                    )
+
+        def empty(p, i):
+            if not 0 <= p < PAIRS:
+                return
+            q = 2 * p + i
+            if p not in xt:
+                grouped = work.tile([P, 2, E], BF16, name="xt", bufs=SB, align_bytes=64)
+                xt[p] = grouped
+            bank = banks.pop(q)
+            dst = xt[p][:, i, :]
+            if kind_of(q) == "pre":
+                nc.scalar.copy(
+                    out=dst.bitcast(F32).rearrange("p (g n u) -> p g n u", g=2, u=2),
+                    in_=bank[:].rearrange("p (u g n) -> p g n u", g=2, u=2),
+                )
+            else:
+                nc.vector.tensor_tensor(
+                    out=dst.rearrange("p (g n u e) -> p g n u e", g=2, u=2, e=2),
+                    in0=bank[:].bitcast(BF16).rearrange("p (u g n e) -> p g n u e", g=2, u=2, e=2),
+                    in1=scale_k[:].rearrange("p g (u e) -> p g u e", u=2).unsqueeze(2).to_broadcast([P, 2, P, 2, 2]),
+                    op=ALU.mult,
+                )
+
+        def quant_x(p, i):
+            if not 0 <= p < PAIRS or (i == 1 and p not in SPLIT):
+                return
+            if p not in xc:
+                codes = work.tile([P, 512], U32, name="xc", bufs=SB, align_bytes=64)
+                scales = work.tile([P, 512], U8, name="xcs", bufs=SB, align_bytes=64)
+                xc[p] = (codes, scales)
+            codes, scales = xc[p]
+            lo, hi = (i, i + 1) if p in SPLIT else (0, 2)
+            c = slice(256 * lo, 256 * hi)
+            nc.vector.quantize_mx(out=codes[:, c].bitcast(F8X4), scales=scales[:, c], in_=xt[p][:, lo:hi, :].rearrange("p i k -> p (i k)"))
+
+        def first_matmul(p, i):
+            if not 0 <= p < PAIRS:
+                return
+            codes, scales = xc[p]
+            bank = psum.tile([P, 512], F32, name="mm1", bufs=2)
+            m1[(p, i)] = bank
+            for t in range(4):
+                for g in range(2):
+                    w = slice(128 * t, 128 * (t + 1))
+                    c = slice(256 * i + 128 * g, 256 * i + 128 * (g + 1))
+                    nc.tensor.matmul_mx(
+                        out=bank[:, 128 * t : 128 * (t + 1)],
+                        lhsT=wa_codes[:, g, w].bitcast(F8X4),
+                        lhsT_scale=wa_scales[:, g, w],
+                        rhs=codes[:, c].bitcast(F8X4),
+                        rhs_scale=scales[:, c],
+                        start=(g == 0),
+                        stop=(g == 1),
+                    )
+
+        def cq_out(p, i):
+            if not 0 <= p < PAIRS:
+                return
+            if p not in cg:
+                grouped = work.tile([P, 2, 512], BF16, name="cg", bufs=SB, align_bytes=64)
+                cg[p] = grouped
+            nc.scalar.copy(
+                out=cg[p][:, i, :].rearrange("p (n t) -> p n t", t=4),
+                in_=m1.pop((p, i))[:].rearrange("p (t n) -> p n t", t=4),
+            )
+
+        def quant_c(p, i):
+            if not 0 <= p < PAIRS or (i == 1 and p not in SPLIT):
+                return
+            if p not in cc:
+                codes = work.tile([P, 256], U32, name="cc", bufs=SB, align_bytes=64)
+                scales = work.tile([P, 256], U8, name="ccs", bufs=SB, align_bytes=64)
+                cc[p] = (codes, scales)
+            codes, scales = cc[p]
+            lo, hi = (i, i + 1) if p in SPLIT else (0, 2)
+            c = slice(128 * lo, 128 * hi)
+            nc.vector.quantize_mx(out=codes[:, c].bitcast(F8X4), scales=scales[:, c], in_=cg[p][:, lo:hi, :].rearrange("p i k -> p (i k)"))
+
+        def second_matmul(p, i):
+            if not 0 <= p < PAIRS:
+                return
+            codes, scales = cc[p]
+            if p not in nope_ps:
+                nb = psum.tile([P, 512], F32, name="nope", bufs=1)
+                rb = psum.tile([P, 256], F32, name="rope", bufs=1)
+                nope_ps[p], rope_ps[p] = nb, rb
+            for bank, width, first in ((nope_ps[p], 256, 0), (rope_ps[p], 128, 256)):
+                t = slice(128 * i, 128 * (i + 1))
+                w = slice(first, first + width)
+                nc.tensor.matmul_mx(
+                    out=bank[:, width * i : width * (i + 1)],
+                    lhsT=codes[:, t].bitcast(F8X4),
+                    lhsT_scale=scales[:, t],
+                    rhs=wb_codes[:, w].bitcast(F8X4),
+                    rhs_scale=wb_scales[:, w],
+                    start=True,
+                    stop=True,
+                )
+
+        def out_tile(p):
+            if p // 2 not in outs:
+                o = work.tile([P, H, 4, QH], F32, name="o", bufs=3, align_bytes=64)
+                outs[p // 2] = o
+            return outs[p // 2]
+
+        def nope_out(p):
+            if not 0 <= p < PAIRS:
+                return
+            jj = 2 * (p % 2)
+            nc.scalar.copy(
+                out=out_tile(p)[:, :, jj : jj + 2, 0:NOPE].rearrange("p h j f -> p j h f"),
+                in_=nope_ps.pop(p)[:].rearrange("p (j h f) -> p j h f", j=2, h=H),
+            )
+
+        def rope_get(p):
+            if 0 <= p < PAIRS and mul_engine(p) != "vector":
+                r = work.tile([P, 256], F32, name="rsb", bufs=SB)
+                nc.vector.tensor_copy(out=r[:], in_=rope_ps.pop(p)[:])
+                rope_sb[p] = r
+
+        def mul_engine(p):
+            return "vector"
+
+        def add_engine(p):
+            return "vector" if p >= PAIRS - 2 else "pool"
+
+        def rope_mul(p):
+            if not 0 <= p < PAIRS:
+                return
+            eng = nc.vector if mul_engine(p) == "vector" else nc.gpsimd
+            t = work.tile([P, 2, 256], F32, name="rcs", bufs=SB)
+            q = (rope_ps if mul_engine(p) == "vector" else rope_sb).pop(p)[:].unsqueeze(1).to_broadcast([P, 2, 256])
+            eng.tensor_tensor(out=t[:], in0=q, in1=table[:, p % 4], op=ALU.mult)
+            rot[p] = t
+
+        def rope_add(p):
+            if not 0 <= p < PAIRS:
+                return
+            eng = nc.vector if add_engine(p) == "vector" else nc.gpsimd
+            jj = 2 * (p % 2)
+            t = rot.pop(p)
+            eng.tensor_tensor(
+                out=out_tile(p)[:, :, jj : jj + 2, NOPE:QH].rearrange("p h j (i e) -> p j h i e", e=2),
+                in0=t[:, 0].rearrange("p (j h i e) -> p j h i e", j=2, h=H, e=2),
+                in1=t[:, 1].rearrange("p (j h i e) -> p j h i e", j=2, h=H, e=2)[:, :, :, :, ::-1],
+                op=ALU.add,
+            )
+
+        def store(p):
+            if not 0 <= p < PAIRS:
+                return
+            b, half = p // 4, (p // 2) % 2
+            dst = out[b].rearrange("h (p j) f -> p h j f", j=J)[:, :, 4 * half : 4 * half + 4, :]
+            if p >= PAIRS - 2:
+                jj = 2 * (p % 2)
+                nc.sync.dma_start(out=dst[:, :, jj : jj + 2, :], in_=out_tile(p)[:, :, jj : jj + 2, :])
+            elif p % 2 == 1:
+                nc.sync.dma_start(out=dst, in_=out_tile(p)[:])
 
         def main():
-            tables_a()
-            for p in range(AHEAD):
-                for i in range(2):
-                    product(p, i)
-            group_wa(0)
-            group_wa(1)
-            tables_b()
-            group_wb()
-            turn(0, 0)
-            turn(0, 1)
-            for s in range(PAIRS + 4):
+            tables_start()
+            for s in range(-4, PAIRS + 4):
+                if s == -3:
+                    group_wa(0, "vector")
+                if s == -3:
+                    group_wa(1, "pool")
+                if s == -1:
+                    tables_end()
+                if s == -3:
+                    group_wb("pool")
                 if s == 1:
-                    quant_wa(0)
-                    quant_wa(1)
+                    quant_wa()
                 if s == 2:
                     quant_wb()
-                if s + 1 < PAIRS:
-                    turn(s + 1, 0)
-                    turn(s + 1, 1)
-                if s < PAIRS:
-                    empty(s, 0)
-                if s + AHEAD < PAIRS:
-                    product(s + AHEAD, 0)
-                if 0 <= s - 1 < PAIRS:
-                    quant_x(s - 1)
-                if 0 <= s - 3 < PAIRS:
-                    nope_out(s - 3)
-                    rope_get(s - 3)
-                    rope_mul(s - 3)
-                    rope_add(s - 3)
-                    if (s - 3) % 2 == 1:
-                        store(s - 3)
-                if s < PAIRS:
-                    empty(s, 1)
-                if s + AHEAD < PAIRS:
-                    product(s + AHEAD, 1)
-                if 0 <= s - 1 < PAIRS:
-                    first_matmul(s - 1)
-                if 0 <= s - 2 < PAIRS:
-                    quant_c(s - 2)
-                    second_matmul(s - 2)
+                turn(s + 3, 0)
+                quant_x(s - 1, 1)
+                cq_out(s - 2, 0)
+                widen(s + 4, 0)
+                turn(s + 3, 1)
+                store(s - 4)
+                rope_get(s - 3)
+                rope_mul(s - 3)
+                cq_out(s - 2, 1)
+                first_matmul(s - 1, 0)
+                empty(s + 2, 0)
+                quant_c(s - 2, 1)
+                widen(s + 4, 1)
+                quant_c(s - 2, 0)
+                empty(s + 3, 1)
+                first_matmul(s - 1, 1)
+                nope_out(s - 3)
+                second_matmul(s - 2, 1)
+                quant_x(s, 0)
+                rope_add(s - 3)
+                second_matmul(s - 2, 0)
+
 
         with tc.manual_schedule():
             main()

@@ -27,10 +27,6 @@ SPLIT = (PAIRS - 1,)
 
 
 def kind_of(q):
-    if q < 4:
-        return "vec" if q % 2 == 0 else "act"
-    if q >= 10 and q % 8 == 2:
-        return "pre"
     return "act"
 
 
@@ -54,7 +50,6 @@ def tile_multilatentattention_pa_t_kernel(tc, x_bytes, x_scale, Wqa, Wqb, out):
         wb_raw = keep.tile([P, 4, H * QH], BF16, name="wb_raw", align_bytes=64)
         wa_src = Wqa.rearrange("(g p j) c -> g p j c", p=P, j=4)
         scale_k = keep.tile([P, 2, 4], F32, name="scale_k")
-        scale_b = keep.tile([P, E], F32, name="scale_b", align_bytes=64)
         load_x(0, 0, 1)
         load_x(0, 1, 2)
         nc.sync.dma_start(out=scale_k[:], in_=x_scale.rearrange("a b (g p t) -> p (a b g) t", g=2, t=4))
@@ -64,7 +59,6 @@ def tile_multilatentattention_pa_t_kernel(tc, x_bytes, x_scale, Wqa, Wqb, out):
         load_x(1, 0, 4)
         nc.sync.dma_start(out=wb_raw[:], in_=Wqb.rearrange("(p j) c -> p j c", j=4))
         load_x(2, 0, 4)
-        nc.sync.dma_start(out=scale_b[:], in_=x_scale.rearrange("a b k -> (a b k)").partition_broadcast(P))
         for hb in range(3, 2 * B):
             load_x(hb, 0, 4)
 
@@ -93,6 +87,8 @@ def tile_multilatentattention_pa_t_kernel(tc, x_bytes, x_scale, Wqa, Wqb, out):
             nc.vector.tensor_tensor(out=frac[:], in0=turns[:], in1=whole[:], op=ALU.subtract)
             nc.vector.scalar_tensor_tensor(out=comp[:], in0=frac[:], scalar=-1.0, in1=frac[:], op0=ALU.mult, op1=ALU.max)
             nc.vector.tensor_scalar(out=comp2[:], in0=comp[:], scalar1=-1.0, scalar2=0.5, op0=ALU.mult, op1=ALU.add)
+
+        def tables_sin():
             nc.scalar.activation(out=half_sin[:], in_=frac[:], func=ACT.Sin, scale=math.pi)
             nc.scalar.activation(out=half_cos[:], in_=comp2[:], func=ACT.Sin, scale=math.pi)
 
@@ -156,9 +152,7 @@ def tile_multilatentattention_pa_t_kernel(tc, x_bytes, x_scale, Wqa, Wqb, out):
             t = work.tile([P, E], BF16, name="xs", bufs=12, align_bytes=64)
             xs[q] = t
             raw = xb[p // 2][:, 2 * (p % 2) + i, :].bitcast(F8)
-            if kind_of(q) == "pre":
-                nc.vector.tensor_tensor(out=t[:], in0=raw, in1=scale_b[:], op=ALU.mult)
-            elif kind_of(q) == "vec":
+            if kind_of(q) == "vec":
                 nc.vector.tensor_copy(out=t[:], in_=raw)
             elif kind_of(q) == "pool":
                 nc.gpsimd.tensor_copy(out=t[:], in_=raw)
@@ -296,11 +290,11 @@ def tile_multilatentattention_pa_t_kernel(tc, x_bytes, x_scale, Wqa, Wqb, out):
         def rope_get(p):
             if 0 <= p < PAIRS and mul_engine(p) != "vector":
                 r = work.tile([P, 256], F32, name="rsb", bufs=SB)
-                nc.vector.tensor_copy(out=r[:], in_=rope_ps.pop(p)[:])
+                nc.scalar.copy(out=r[:], in_=rope_ps.pop(p)[:])
                 rope_sb[p] = r
 
         def mul_engine(p):
-            return "vector"
+            return "pool" if p < PAIRS - 2 else "vector"
 
         def add_engine(p):
             return "vector" if p >= PAIRS - 2 else "pool"
@@ -340,41 +334,42 @@ def tile_multilatentattention_pa_t_kernel(tc, x_bytes, x_scale, Wqa, Wqb, out):
 
         def main():
             tables_start()
-            for s in range(-4, PAIRS + 4):
-                if s == -3:
+            for s in range(-44, PAIRS + 4):
+                if s == -2:
                     group_wa(0, "vector")
-                if s == -3:
+                if s == 0:
                     group_wa(1, "pool")
-                if s == -1:
+                if s == -44:
+                    tables_sin()
+                if s == 0:
                     tables_end()
-                if s == -3:
+                if s == 0:
                     group_wb("pool")
-                if s == 1:
+                if s == 0:
                     quant_wa()
                 if s == 2:
                     quant_wb()
-                turn(s + 3, 0)
-                quant_x(s - 1, 1)
-                cq_out(s - 2, 0)
-                widen(s + 4, 0)
-                turn(s + 3, 1)
+                rope_add(s - 3)
+                widen(s + 2, 1)
+                second_matmul(s - 2, 0)
+                widen(s + 3, 0)
+                empty(s + 1, 0)
                 store(s - 4)
-                rope_get(s - 3)
-                rope_mul(s - 3)
-                cq_out(s - 2, 1)
-                first_matmul(s - 1, 0)
-                empty(s + 2, 0)
-                quant_c(s - 2, 1)
-                widen(s + 4, 1)
-                quant_c(s - 2, 0)
-                empty(s + 3, 1)
-                first_matmul(s - 1, 1)
-                nope_out(s - 3)
+                cq_out(s - 1, 0)
+                cq_out(s - 1, 1)
                 second_matmul(s - 2, 1)
                 quant_x(s, 0)
-                rope_add(s - 3)
-                second_matmul(s - 2, 0)
-
+                rope_get(s - 2)
+                turn(s + 2, 0)
+                nope_out(s - 2)
+                empty(s + 1, 1)
+                quant_x(s, 1)
+                turn(s + 2, 1)
+                first_matmul(s, 0)
+                rope_mul(s - 2)
+                quant_c(s - 1, 0)
+                first_matmul(s, 1)
+                quant_c(s - 1, 1)
 
         with tc.manual_schedule():
             main()

import math
from contextlib import ExitStack

import concourse.mybir as mybir
from concourse.masks import make_identity

B, N, E, H, NOPE, ROPE, QR = 4, 1024, 1024, 4, 64, 32, 512
QH = NOPE + ROPE
BASE = 10000.0
FLOPS = 2 * B * N * E * QR + 2 * B * N * QR * H * QH + 6 * B * N * H * ROPE // 2

F32 = mybir.dt.float32
BF16 = mybir.dt.bfloat16
I32 = mybir.dt.int32
U32 = mybir.dt.uint32
U8 = mybir.dt.uint8
F8 = mybir.dt.float8_e4m3fn
F8X4 = mybir.dt.float8_e4m3fn_x4
ALU = mybir.AluOpType
ACT = mybir.ActivationFunctionType

P = 128
J = N // P
PAIRS = B * J // 2
SB = 4
SPLIT = (PAIRS - 1,)


def kind_of(q):
    return "act"


def tile_multilatentattention_pa_t_kernel(tc, x_bytes, x_scale, Wqa, Wqb, out):
    nc = tc.nc
    with ExitStack() as ctx:
        keep = ctx.enter_context(tc.tile_pool(name="keep", bufs=1))
        work = ctx.enter_context(tc.tile_pool(name="work", bufs=2))
        psum = ctx.enter_context(tc.psum_pool(name="psum", bufs=2))

        xb = []
        for hb in range(2 * B):
            xb.append(keep.tile([P, 4, E], U8, name="xb%d" % hb, align_bytes=64))

        def load_x(hb, lo, hi):
            src = x_bytes[hb // 2].rearrange("(p j) k -> p j k", j=J)
            first = 4 * (hb % 2)
            nc.sync.dma_start(out=xb[hb][:, lo:hi, :], in_=src[:, first + lo : first + hi, :])

        wa_raw = keep.tile([P, 2, 4, QR], BF16, name="wa_raw", align_bytes=64)
        wb_raw = keep.tile([P, 4, H * QH], BF16, name="wb_raw", align_bytes=64)
        wa_src = Wqa.rearrange("(g p j) c -> g p j c", p=P, j=4)
        scale_k = keep.tile([P, 2, 4], F32, name="scale_k")
        load_x(0, 0, 1)
        load_x(0, 1, 2)
        nc.sync.dma_start(out=scale_k[:], in_=x_scale.rearrange("a b (g p t) -> p (a b g) t", g=2, t=4))
        nc.sync.dma_start(out=wa_raw[:, 0], in_=wa_src[0])
        load_x(0, 2, 4)
        nc.sync.dma_start(out=wa_raw[:, 1], in_=wa_src[1])
        load_x(1, 0, 4)
        nc.sync.dma_start(out=wb_raw[:], in_=Wqb.rearrange("(p j) c -> p j c", j=4))
        load_x(2, 0, 4)
        for hb in range(3, 2 * B):
            load_x(hb, 0, 4)

        pos = keep.tile([P, J], F32, name="pos")
        ident = keep.tile([P, P], F32, name="ident", align_bytes=64)
        turns = keep.tile([P, J, 16], F32, name="turns")
        whole_i = keep.tile([P, J, 16], I32, name="whole_i")
        whole = keep.tile([P, J, 16], F32, name="whole")
        frac = keep.tile([P, J, 16], F32, name="frac")
        comp = keep.tile([P, J, 16], F32, name="comp")
        comp2 = keep.tile([P, J, 16], F32, name="comp2")
        half_sin = keep.tile([P, J, 16], F32, name="half_sin")
        half_cos = keep.tile([P, J, 16], F32, name="half_cos")
        sc = keep.tile([P, J, 16], F32, name="sc")
        ss = keep.tile([P, J, 16], F32, name="ss")
        table = keep.tile([P, J // 2, 2, 2 * H * ROPE], F32, name="table", align_bytes=64)

        def tables_start():
            nc.gpsimd.iota(pos[:], pattern=[[1, J]], base=0, channel_multiplier=J, allow_small_or_imprecise_dtypes=True)
            make_identity(nc, ident[:])
            for i in range(16):
                theta = BASE ** (-2.0 * i / ROPE)
                nc.vector.tensor_scalar(out=turns[:, :, i], in0=pos[:], scalar1=theta / (2.0 * math.pi), scalar2=None, op0=ALU.mult)
            nc.vector.tensor_copy(out=whole_i[:], in_=turns[:])
            nc.vector.tensor_copy(out=whole[:], in_=whole_i[:])
            nc.vector.tensor_tensor(out=frac[:], in0=turns[:], in1=whole[:], op=ALU.subtract)
            nc.vector.scalar_tensor_tensor(out=comp[:], in0=frac[:], scalar=-1.0, in1=frac[:], op0=ALU.mult, op1=ALU.max)
            nc.vector.tensor_scalar(out=comp2[:], in0=comp[:], scalar1=-1.0, scalar2=0.5, op0=ALU.mult, op1=ALU.add)

        def tables_sin():
            nc.scalar.activation(out=half_sin[:], in_=frac[:], func=ACT.Sin, scale=math.pi)
            nc.scalar.activation(out=half_cos[:], in_=comp2[:], func=ACT.Sin, scale=math.pi)

        def tables_end():
            nc.gpsimd.tensor_tensor(out=sc[:], in0=half_sin[:], in1=half_cos[:], op=ALU.mult)
            nc.gpsimd.tensor_tensor(out=ss[:], in0=half_sin[:], in1=half_sin[:], op=ALU.mult)
            for e in range(2):
                for d in range(2):
                    for c, part, mul, add in ((0, ss, -2.0, 1.0), (1, sc, 2.0 - 4.0 * e, 0.0)):
                        nc.gpsimd.tensor_scalar(
                            out=table[:, :, c, :].rearrange("p m (d h i e) -> p d e m h i", d=2, h=H, e=2)[:, d, e],
                            in0=part[:].rearrange("p (m d) i -> p d m i", d=2)[:, d].unsqueeze(2).to_broadcast([P, J // 2, H, 16]),
                            scalar1=mul,
                            scalar2=add,
                            op0=ALU.mult,
                            op1=ALU.add,
                        )

        wa_grp = keep.tile([P, 2, 2048], BF16, name="wa_grp", align_bytes=64)
        wa_codes = keep.tile([P, 2, QR], U32, name="wa_codes", align_bytes=64)
        wa_scales = keep.tile([P, 2, QR], U8, name="wa_scales", align_bytes=64)
        wb_grp = keep.tile([P, H * QH * 4], BF16, name="wb_grp", align_bytes=64)
        wb_codes = keep.tile([P, H * QH], U32, name="wb_codes", align_bytes=64)
        wb_scales = keep.tile([P, H * QH], U8, name="wb_scales", align_bytes=64)

        def copy_on(engine, dst, src):
            if engine == "vector":
                nc.vector.tensor_copy(out=dst, in_=src)
            elif engine == "scalar":
                nc.scalar.copy(out=dst, in_=src)
            else:
                nc.gpsimd.tensor_scalar(out=dst, in0=src, scalar1=1.0, scalar2=0.0, op0=ALU.mult, op1=ALU.add)

        def group_wa(g, engine):
            copy_on(
                engine,
                wa_grp[:, g, :].rearrange("p (t m j) -> p t m j", t=4, j=4),
                wa_raw[:, g].rearrange("p j (m t) -> p t m j", t=4),
            )

        def quant_wa():
            for g in range(2):
                nc.vector.quantize_mx(out=wa_codes[:, g, :].bitcast(F8X4), scales=wa_scales[:, g, :], in_=wa_grp[:, g, :])

        def group_wb(engine):
            raw = wb_raw[:].rearrange("p j (h f) -> p h f j", h=H)
            copy_on(engine, wb_grp[:, 0:1024].rearrange("p (h f j) -> p h f j", h=H, j=4), raw[:, :, 0:NOPE, :])
            copy_on(engine, wb_grp[:, 1024:1536].rearrange("p (h f j) -> p h f j", h=H, j=4), raw[:, :, NOPE:QH, :])

        def quant_wb():
            nc.vector.quantize_mx(out=wb_codes[:, 0:256].bitcast(F8X4), scales=wb_scales[:, 0:256], in_=wb_grp[:, 0:1024])
            nc.vector.quantize_mx(out=wb_codes[:, 256:384].bitcast(F8X4), scales=wb_scales[:, 256:384], in_=wb_grp[:, 1024:1536])

        xs, banks, xt, xc, cg, cc, nope_ps, rope_ps, rope_sb, rot, outs = {}, {}, {}, {}, {}, {}, {}, {}, {}, {}, {}
        m1 = {}

        def widen(p, i):
            if not 0 <= p < PAIRS:
                return
            q = 2 * p + i
            t = work.tile([P, E], BF16, name="xs", bufs=12, align_bytes=64)
            xs[q] = t
            raw = xb[p // 2][:, 2 * (p % 2) + i, :].bitcast(F8)
            if kind_of(q) == "vec":
                nc.vector.tensor_copy(out=t[:], in_=raw)
            elif kind_of(q) == "pool":
                nc.gpsimd.tensor_copy(out=t[:], in_=raw)
            else:
                nc.scalar.copy(out=t[:], in_=raw)

        def turn(p, i):
            if not 0 <= p < PAIRS:
                return
            q = 2 * p + i
            words = xs.pop(q)[:].bitcast(F32)
            bank = psum.tile([P, 512], F32, name="tp", bufs=4)
            banks[q] = bank
            for g in range(2):
                for u in range(2):
                    nc.tensor.transpose(
                        bank[:, 128 * (2 * u + g) : 128 * (2 * u + g + 1)],
                        words[:, 256 * g + u : 256 * (g + 1) : 2],
                        ident[:],
                    )

        def empty(p, i):
            if not 0 <= p < PAIRS:
                return
            q = 2 * p + i
            if p not in xt:
                grouped = work.tile([P, 2, E], BF16, name="xt", bufs=SB, align_bytes=64)
                xt[p] = grouped
            bank = banks.pop(q)
            dst = xt[p][:, i, :]
            if kind_of(q) == "pre":
                nc.scalar.copy(
                    out=dst.bitcast(F32).rearrange("p (g n u) -> p g n u", g=2, u=2),
                    in_=bank[:].rearrange("p (u g n) -> p g n u", g=2, u=2),
                )
            else:
                nc.vector.tensor_tensor(
                    out=dst.rearrange("p (g n u e) -> p g n u e", g=2, u=2, e=2),
                    in0=bank[:].bitcast(BF16).rearrange("p (u g n e) -> p g n u e", g=2, u=2, e=2),
                    in1=scale_k[:].rearrange("p g (u e) -> p g u e", u=2).unsqueeze(2).to_broadcast([P, 2, P, 2, 2]),
                    op=ALU.mult,
                )

        def quant_x(p, i):
            if not 0 <= p < PAIRS or (i == 1 and p not in SPLIT):
                return
            if p not in xc:
                codes = work.tile([P, 512], U32, name="xc", bufs=SB, align_bytes=64)
                scales = work.tile([P, 512], U8, name="xcs", bufs=SB, align_bytes=64)
                xc[p] = (codes, scales)
            codes, scales = xc[p]
            lo, hi = (i, i + 1) if p in SPLIT else (0, 2)
            c = slice(256 * lo, 256 * hi)
            nc.vector.quantize_mx(out=codes[:, c].bitcast(F8X4), scales=scales[:, c], in_=xt[p][:, lo:hi, :].rearrange("p i k -> p (i k)"))

        def first_matmul(p, i):
            if not 0 <= p < PAIRS:
                return
            codes, scales = xc[p]
            bank = psum.tile([P, 512], F32, name="mm1", bufs=2)
            m1[(p, i)] = bank
            for t in range(4):
                for g in range(2):
                    w = slice(128 * t, 128 * (t + 1))
                    c = slice(256 * i + 128 * g, 256 * i + 128 * (g + 1))
                    nc.tensor.matmul_mx(
                        out=bank[:, 128 * t : 128 * (t + 1)],
                        lhsT=wa_codes[:, g, w].bitcast(F8X4),
                        lhsT_scale=wa_scales[:, g, w],
                        rhs=codes[:, c].bitcast(F8X4),
                        rhs_scale=scales[:, c],
                        start=(g == 0),
                        stop=(g == 1),
                    )

        def cq_out(p, i):
            if not 0 <= p < PAIRS:
                return
            if p not in cg:
                grouped = work.tile([P, 2, 512], BF16, name="cg", bufs=SB, align_bytes=64)
                cg[p] = grouped
            nc.scalar.copy(
                out=cg[p][:, i, :].rearrange("p (n t) -> p n t", t=4),
                in_=m1.pop((p, i))[:].rearrange("p (t n) -> p n t", t=4),
            )

        def quant_c(p, i):
            if not 0 <= p < PAIRS or (i == 1 and p not in SPLIT):
                return
            if p not in cc:
                codes = work.tile([P, 256], U32, name="cc", bufs=SB, align_bytes=64)
                scales = work.tile([P, 256], U8, name="ccs", bufs=SB, align_bytes=64)
                cc[p] = (codes, scales)
            codes, scales = cc[p]
            lo, hi = (i, i + 1) if p in SPLIT else (0, 2)
            c = slice(128 * lo, 128 * hi)
            nc.vector.quantize_mx(out=codes[:, c].bitcast(F8X4), scales=scales[:, c], in_=cg[p][:, lo:hi, :].rearrange("p i k -> p (i k)"))

        def second_matmul(p, i):
            if not 0 <= p < PAIRS:
                return
            codes, scales = cc[p]
            if p not in nope_ps:
                nb = psum.tile([P, 512], F32, name="nope", bufs=1)
                rb = psum.tile([P, 256], F32, name="rope", bufs=1)
                nope_ps[p], rope_ps[p] = nb, rb
            for bank, width, first in ((nope_ps[p], 256, 0), (rope_ps[p], 128, 256)):
                t = slice(128 * i, 128 * (i + 1))
                w = slice(first, first + width)
                nc.tensor.matmul_mx(
                    out=bank[:, width * i : width * (i + 1)],
                    lhsT=codes[:, t].bitcast(F8X4),
                    lhsT_scale=scales[:, t],
                    rhs=wb_codes[:, w].bitcast(F8X4),
                    rhs_scale=wb_scales[:, w],
                    start=True,
                    stop=True,
                )

        def out_tile(p):
            if p // 2 not in outs:
                o = work.tile([P, H, 4, QH], F32, name="o", bufs=3, align_bytes=64)
                outs[p // 2] = o
            return outs[p // 2]

        def nope_out(p):
            if not 0 <= p < PAIRS:
                return
            jj = 2 * (p % 2)
            nc.scalar.copy(
                out=out_tile(p)[:, :, jj : jj + 2, 0:NOPE].rearrange("p h j f -> p j h f"),
                in_=nope_ps.pop(p)[:].rearrange("p (j h f) -> p j h f", j=2, h=H),
            )

        def rope_get(p):
            if 0 <= p < PAIRS and mul_engine(p) != "vector":
                r = work.tile([P, 256], F32, name="rsb", bufs=SB)
                nc.scalar.copy(out=r[:], in_=rope_ps.pop(p)[:])
                rope_sb[p] = r

        def mul_engine(p):
            return "pool" if p < PAIRS - 2 else "vector"

        def add_engine(p):
            return "vector" if p >= PAIRS - 2 else "pool"

        def rope_mul(p):
            if not 0 <= p < PAIRS:
                return
            eng = nc.vector if mul_engine(p) == "vector" else nc.gpsimd
            t = work.tile([P, 2, 256], F32, name="rcs", bufs=SB)
            q = (rope_ps if mul_engine(p) == "vector" else rope_sb).pop(p)[:].unsqueeze(1).to_broadcast([P, 2, 256])
            eng.tensor_tensor(out=t[:], in0=q, in1=table[:, p % 4], op=ALU.mult)
            rot[p] = t

        def rope_add(p):
            if not 0 <= p < PAIRS:
                return
            eng = nc.vector if add_engine(p) == "vector" else nc.gpsimd
            jj = 2 * (p % 2)
            t = rot.pop(p)
            eng.tensor_tensor(
                out=out_tile(p)[:, :, jj : jj + 2, NOPE:QH].rearrange("p h j (i e) -> p j h i e", e=2),
                in0=t[:, 0].rearrange("p (j h i e) -> p j h i e", j=2, h=H, e=2),
                in1=t[:, 1].rearrange("p (j h i e) -> p j h i e", j=2, h=H, e=2)[:, :, :, :, ::-1],
                op=ALU.add,
            )

        def store(p):
            if not 0 <= p < PAIRS:
                return
            b, half = p // 4, (p // 2) % 2
            dst = out[b].rearrange("h (p j) f -> p h j f", j=J)[:, :, 4 * half : 4 * half + 4, :]
            if p >= PAIRS - 2:
                jj = 2 * (p % 2)
                nc.sync.dma_start(out=dst[:, :, jj : jj + 2, :], in_=out_tile(p)[:, :, jj : jj + 2, :])
            elif p % 2 == 1:
                nc.sync.dma_start(out=dst, in_=out_tile(p)[:])

        def main():
            tables_start()
            for s in range(-44, PAIRS + 4):
                if s == -2:
                    group_wa(0, "vector")
                if s == 0:
                    group_wa(1, "pool")
                if s == -44:
                    tables_sin()
                if s == 0:
                    tables_end()
                if s == 0:
                    group_wb("pool")
                if s == 0:
                    quant_wa()
                if s == 2:
                    quant_wb()
                rope_add(s - 3)
                widen(s + 2, 1)
                second_matmul(s - 2, 0)
                widen(s + 3, 0)
                empty(s + 1, 0)
                store(s - 4)
                cq_out(s - 1, 0)
                cq_out(s - 1, 1)
                second_matmul(s - 2, 1)
                quant_x(s, 0)
                rope_get(s - 2)
                turn(s + 2, 0)
                nope_out(s - 2)
                empty(s + 1, 1)
                quant_x(s, 1)
                turn(s + 2, 1)
                first_matmul(s, 0)
                rope_mul(s - 2)
                quant_c(s - 1, 0)
                first_matmul(s, 1)
                quant_c(s - 1, 1)

        with tc.manual_schedule():
            main()
